import numpy as np
import ml_dtypes


def mxq(x, axis, fmt="e4m3"):
    dtype, down = {"e4m3": (ml_dtypes.float8_e4m3fn, 7), "e5m2": (ml_dtypes.float8_e5m2, 14)}[fmt]
    v = np.moveaxis(np.asarray(x, np.float32).astype(ml_dtypes.bfloat16).astype(np.float64), axis, -1)
    blocks = v.reshape(v.shape[:-1] + (-1, 32))
    amax = np.abs(blocks).max(-1, keepdims=True)
    byte = np.maximum(np.where(amax > 0, np.frexp(amax)[1] - 1 + 127, 0) - down, 1)
    scale = np.exp2(byte - 127.0)
    codes = (blocks / scale).astype(np.float32).astype(dtype).astype(np.float64)
    return np.moveaxis((codes * scale).reshape(v.shape), -1, axis)


WIDE = False


def mx_kscale(k):
    if not WIDE:
        return np.ones(k)
    levels = np.array([10, -10, 5, -5, 0])
    if k % 512:
        return np.exp2(np.random.permutation(np.resize(levels, k // 32))).repeat(32)
    a = np.empty((k // 512, 16))
    for p in range(k // 512):
        a[p, :8] = np.random.permutation(np.resize(levels, 8))
        for g in range(8):
            far = levels[np.abs(levels - a[p, g]) >= 10]
            a[p, g + 8] = far[np.random.randint(len(far))]
    return np.exp2(a.ravel()).repeat(32)


BF16 = ml_dtypes.bfloat16


def bf(x):
    return np.asarray(x, np.float32).astype(BF16)


def f64(x):
    return np.asarray(x).astype(np.float64)


N, IN, HID, OUT, MLP, NF = 8192, 256, 512, 128, 512, 8
FS = N // NF


def draw_hiddens():
    amp = 0.2 + 0.8 * np.random.random((N, 1))
    centre = np.repeat(np.random.standard_normal((NF, HID)), FS, axis=0)
    return amp * np.random.standard_normal((N, HID)) + 0.3 * centre


def draw0():
    s, t = mx_kscale(HID), mx_kscale(MLP)
    c1 = 1.2 / np.sqrt(IN + HID)
    cx = 1.2 * np.sqrt(IN / (IN + HID))
    c2 = 2.0 / np.sqrt(MLP)
    return {
        "hiddens": bf(draw_hiddens() * s),
        "Wa1h": bf(np.random.standard_normal((MLP, HID)) * c1 * t[:, None] / s),
        "drive_a": bf(np.random.standard_normal(MLP) * cx * t),
        "Wa2": bf(np.random.standard_normal((OUT, MLP)) * c2 / t),
        "ba2": bf(np.random.standard_normal(OUT) * 0.1),
        "Wg1h": bf(np.random.standard_normal((MLP, HID)) * c1 * t[:, None] / s),
        "drive_g": bf(np.random.standard_normal(MLP) * cx * t),
        "Wg2": bf(np.random.standard_normal((OUT, MLP)) * c2 / t),
        "bg2": bf(np.random.standard_normal(OUT) * 0.1),
    }


def engine(hq, w1h, drive, w2, b2):
    u = np.maximum((hq @ mxq(f64(w1h), 1, "e4m3").T) + f64(drive), 0.0)
    return (mxq(u, 1, "e4m3") @ mxq(f64(w2), 1, "e4m3").T) + f64(b2)


def core(hiddens, Wa1h, drive_a, Wa2, ba2, Wg1h, drive_g, Wg2, bg2):
    hq = mxq(f64(hiddens), 1, "e4m3")
    a = engine(hq, Wa1h, drive_a, Wa2, ba2)
    g = engine(hq, Wg1h, drive_g, Wg2, bg2)
    diff = a - g
    tension = np.mean(diff * diff, axis=-1, keepdims=True)
    t0 = tension[:, 0]
    e = np.exp(t0 - t0.max())
    w = e / e.sum()
    combined = (w[:, None] * diff).sum(axis=0, keepdims=True)
    mean_tension = tension.mean(axis=0)
    return diff, tension, combined, mean_tension


def e4m3fn_bytes(y):
    return np.clip(np.asarray(y, np.float64), -448.0, 448.0).astype(np.float32).astype(ml_dtypes.float8_e4m3fn).view(np.uint8)


def e4m3fn_values(b):
    return np.asarray(b, np.uint8).view(ml_dtypes.float8_e4m3fn).astype(np.float64)


def setup_inputs():
    d = draw0()
    x0 = np.asarray(d['hiddens']).astype(np.float64)
    s = (np.max(np.abs(x0), axis=(0,), keepdims=True) / 448.0).astype(np.float32)
    out = {}
    for k, v in d.items():
        if k == 'hiddens':
            out['hiddens_bytes'] = e4m3fn_bytes(x0 / s.astype(np.float64))
            out['hiddens_scale'] = s
        else:
            out[k] = v
    return out


def reference(hiddens_bytes, hiddens_scale, Wa1h, drive_a, Wa2, ba2, Wg1h, drive_g, Wg2, bg2):
    return core(e4m3fn_values(hiddens_bytes) * hiddens_scale.astype(np.float64), Wa1h, drive_a, Wa2, ba2, Wg1h, drive_g, Wg2, bg2)

@@ -1,0 +1,388 @@
+from contextlib import ExitStack
+
+import concourse.mybir as mybir
+from concourse.masks import make_identity
+
+F32 = mybir.dt.float32
+BF16 = mybir.dt.bfloat16
+U32 = mybir.dt.uint32
+U8 = mybir.dt.uint8
+FP8 = mybir.dt.float8_e4m3fn
+FP8X4 = mybir.dt.float8_e4m3fn_x4
+ADD = mybir.AluOpType.add
+SUB = mybir.AluOpType.subtract
+MULT = mybir.AluOpType.mult
+MAX = mybir.AluOpType.max
+ACT = mybir.ActivationFunctionType
+X = mybir.AxisListType.X
+
+P = 128
+N, K, HID, OUT = 8192, 512, 512, 128
+Q = N // P
+SIZES = [2] + [4] * 15 + [2]
+NC = len(SIZES)
+T0 = [sum(SIZES[:c]) for c in range(NC)]
+CTM = 4
+WM = CTM * P
+HS = 56
+
+FLOPS = 2 * N * K * 2 * HID + 2 * N * 2 * HID * OUT
+
+
+def tile_phiaslossengine_pa_t_kernel(
+    tc, hiddens_bytes, hiddens_scale, Wa1h, drive_a, Wa2, ba2, Wg1h, drive_g, Wg2, bg2,
+    out_0, out_1, out_2, out_3,
+):
+    nc = tc.nc
+    hb = hiddens_bytes.rearrange("(p q) k -> p (q k)", q=Q)
+    od = out_0.rearrange("(p q) n -> p (q n)", q=Q)
+    ot = out_1.rearrange("(p q) o -> p (q o)", q=Q)
+
+    with ExitStack() as ctx:
+        keep = ctx.enter_context(tc.tile_pool(name="keep", bufs=1))
+        bpool = ctx.enter_context(tc.tile_pool(name="bytes", bufs=NC))
+        xpool = ctx.enter_context(tc.tile_pool(name="x", bufs=3))
+        upool = ctx.enter_context(tc.tile_pool(name="u", bufs=4))
+        dpool = ctx.enter_context(tc.tile_pool(name="d", bufs=NC))
+        small = ctx.enter_context(tc.tile_pool(name="small", bufs=2))
+        tps = ctx.enter_context(tc.psum_pool(name="tps", bufs=2))
+        hps = ctx.enter_context(tc.psum_pool(name="hps", bufs=4))
+        yps = ctx.enter_context(tc.psum_pool(name="yps", bufs=1))
+        cps = ctx.enter_context(tc.psum_pool(name="cps", bufs=1))
+        ctx.enter_context(tc.manual_schedule())
+
+        hbytes = []
+
+        def load(c):
+            hb_t = bpool.tile([P, CTM * K], U8, name="hb_t", align_bytes=64)
+            nc.sync.dma_start(out=hb_t[:, 0:SIZES[c] * K], in_=hb[:, T0[c] * K:(T0[c] + SIZES[c]) * K])
+            hbytes.append(hb_t)
+
+        scale4 = keep.tile([P, CTM * K], F32, name="scale4", align_bytes=64)
+        nc.scalar.dma_start(out=scale4[:, 0:K], in_=hiddens_scale.rearrange("o k -> (o k)").partition_broadcast(P))
+        load(0)
+        w1raw = []
+        for n, w in enumerate((Wa1h, Wg1h)):
+            wr = keep.tile([P, 4 * K], BF16, name="w1raw%d" % n, align_bytes=64)
+            nc.sync.dma_start(out=wr[:].rearrange("p (t k) -> p t k", t=4), in_=w.rearrange("(m t) k -> m t k", t=4))
+            w1raw.append(wr)
+            load(1 + n)
+        dr_raw = []
+        for n, v in enumerate((drive_a, drive_g)):
+            t_ = keep.tile([P, 4], BF16, name="drraw%d" % n)
+            nc.scalar.dma_start(out=t_[:], in_=v.rearrange("(p t) -> p t", t=4))
+            dr_raw.append(t_)
+        w2raw = []
+        for n, w in enumerate((Wa2, Wg2)):
+            wr = keep.tile([P, HID], BF16, name="w2raw%d" % n, align_bytes=64)
+            nc.sync.dma_start(out=wr[:], in_=w)
+            w2raw.append(wr)
+        b_raw = []
+        for n, v in enumerate((ba2, bg2)):
+            t_ = keep.tile([P, OUT], BF16, name="braw%d" % n, align_bytes=64)
+            nc.sync.dma_start(out=t_[:], in_=v.partition_broadcast(P))
+            b_raw.append(t_)
+        for c in range(3, NC):
+            load(c)
+
+        ident = keep.tile([P, P], F32, name="ident", align_bytes=64)
+        make_identity(nc, ident[:])
+        ones = keep.tile([P, P], F32, name="ones", align_bytes=64)
+        nc.gpsimd.memset(ones[:], 1.0)
+        warm = keep.tile([P, 1], F32, name="warm")
+        nc.gpsimd.memset(warm[:], 0.0)
+        warm2 = keep.tile([P, 1], F32, name="warm2")
+        nc.scalar.activation(out=warm2[:], in_=warm[:], func=ACT.Exp)
+
+        ss = keep.tile([P, Q], F32, name="ss", align_bytes=64)
+        e = keep.tile([P, Q], F32, name="e", align_bytes=64)
+
+        xs, xwords, xq, xsc, tp = {}, {}, {}, {}, {}
+        up, ug, uq, us = {}, {}, {}, {}
+        diff = {}
+        w1q, w1s = [None, None], [None, None]
+
+        def B(c, a=None, b=None):
+            n = SIZES[c] * K
+            if not a:
+                xs[c] = xpool.tile([P, CTM * K], BF16, name="xs", align_bytes=64)
+            step = K if c < 2 else n
+            for s in range((a or 0) * K, n if b is None else b * K, step):
+                nc.vector.tensor_tensor(out=xs[c][:, s:s + step], in0=hbytes[c][:, s:s + step].bitcast(FP8),
+                                        in1=scale4[:, 0:step], op=MULT)
+
+        def transpose_words(src, nslots):
+            words = src.bitcast(F32)
+            res = []
+            for h in range(nslots // 2):
+                tp_t = tps.tile([P, 512], F32, name="tp_t")
+                for j in range(2):
+                    for u in range(2):
+                        s = 256 * (2 * h + j)
+                        nc.tensor.transpose(tp_t[:, (2 * j + u) * P:(2 * j + u + 1) * P], words[:, s + u:s + 256:2], ident[:])
+                res.append(tp_t)
+            return res
+
+        def words_out(eng, tp_t, dst):
+            o = dst.bitcast(F32).rearrange("p (j r u) -> p j r u", j=2, u=2)
+            i = tp_t[:].rearrange("p (j u r) -> p j r u", j=2, u=2)
+            if eng == "s":
+                nc.scalar.copy(out=o, in_=i)
+            else:
+                nc.vector.tensor_copy(out=o, in_=i)
+
+        def C(c):
+            tp[c] = transpose_words(xs.pop(c)[:], SIZES[c])
+            xwords[c] = xpool.tile([P, CTM * K], BF16, name="xg", align_bytes=64)
+
+        def D(c, h, eng="s"):
+            if h < len(tp[c]):
+                words_out(eng, tp[c][h], xwords[c][:, h * 1024:(h + 1) * 1024])
+
+        def E(c):
+            w = SIZES[c] * P
+            xq[c] = xpool.tile([P, WM], U32, name="xq", align_bytes=64)
+            xsc[c] = xpool.tile([P, WM], U8, name="xsc", align_bytes=64)
+            nc.vector.quantize_mx(out=xq[c][:, 0:w].bitcast(FP8X4), scales=xsc[c][:, 0:w], in_=xwords.pop(c)[:, 0:4 * w])
+
+        def FG(c, n, t, eng="s"):
+            w = SIZES[c] * P
+            if t == 0:
+                up[c, n] = upool.tile([P, 4 * WM], BF16, name="up", align_bytes=64)
+            h_t = hps.tile([P, WM], F32, name="h_t")
+            nc.tensor.matmul_mx(
+                out=h_t[:, 0:w],
+                lhsT=w1q[n][:, t * P:(t + 1) * P].bitcast(FP8X4), lhsT_scale=w1s[n][:, t * P:(t + 1) * P],
+                rhs=xq[c][:, 0:w].bitcast(FP8X4), rhs_scale=xsc[c][:, 0:w], start=True, stop=True)
+            o = up[c, n][:, t * w:(t + 1) * w]
+            b = dr[:, 4 * n + t:4 * n + t + 1]
+            if eng == "s":
+                nc.scalar.activation(out=o, in_=h_t[:, 0:w], func=ACT.Relu, bias=b)
+            else:
+                nc.vector.tensor_scalar(out=o, in0=h_t[:, 0:w], scalar1=b, scalar2=0.0, op0=ADD, op1=MAX)
+
+        def H(c, n, hs):
+            w = SIZES[c] * P
+            ug[c, n] = upool.tile([P, 4 * WM], BF16, name="ug", align_bytes=64)
+            dst = ug[c, n][:, 0:4 * w].rearrange("p (c i t) -> p c t i", i=4, t=4)
+            src = up.pop((c, n))[:, 0:4 * w].rearrange("p (t c i) -> p c t i", t=4, i=4)
+            cut = (w - hs) // 4
+            if hs:
+                nc.scalar.copy(out=dst[:, cut:w // 4], in_=src[:, cut:w // 4])
+            nc.vector.tensor_copy(out=dst[:, 0:cut], in_=src[:, 0:cut])
+
+        def I(c, n):
+            w = SIZES[c] * P
+            uq[c, n] = upool.tile([P, WM], U32, name="uq", align_bytes=64)
+            us[c, n] = upool.tile([P, WM], U8, name="us", align_bytes=64)
+            nc.vector.quantize_mx(out=uq[c, n][:, 0:w].bitcast(FP8X4), scales=us[c, n][:, 0:w], in_=ug.pop((c, n))[:, 0:4 * w])
+
+        y = {}
+
+        def J(c):
+            y[c] = yps.tile([P, WM], F32, name="y_t")
+            for j in range(SIZES[c]):
+                for n in range(2):
+                    nc.tensor.matmul_mx(
+                        out=y[c][:, j * P:(j + 1) * P],
+                        lhsT=uq[c, n][:, j * P:(j + 1) * P].bitcast(FP8X4), lhsT_scale=us[c, n][:, j * P:(j + 1) * P],
+                        rhs=w2q[:, n * P:(n + 1) * P].bitcast(FP8X4), rhs_scale=w2s[:, n * P:(n + 1) * P],
+                        start=(n == 0), stop=(n == 1))
+
+        def Kk(c):
+            w = SIZES[c] * P
+            diff[c] = dpool.tile([P, WM], F32, name="diff", align_bytes=64)
+            nc.vector.tensor_tensor(
+                out=diff[c][:, 0:w].rearrange("p (j n) -> p j n", n=OUT), in0=y.pop(c)[:, 0:w].rearrange("p (j n) -> p j n", n=OUT),
+                in1=b2[:].unsqueeze(1).to_broadcast([P, SIZES[c], OUT]), op=ADD)
+            nc.sync.dma_start(out=od[:, T0[c] * OUT:(T0[c] + SIZES[c]) * OUT], in_=diff[c][:, 0:w])
+
+        def L(c):
+            for j in range(SIZES[c]):
+                junk = small.tile([P, OUT], F32, name="junk")
+                nc.scalar.activation(out=junk[:], in_=diff[c][:, j * P:(j + 1) * P], func=ACT.Square,
+                                     accum_out=ss[:, T0[c] + j:T0[c] + j + 1])
+
+        groups = [(0, 5), (5, 9), (9, 12), (12, 14), (14, 15), (15, 17)]
+        G = len(groups)
+        gm = keep.tile([P, G], F32, name="gm")
+        nm = keep.tile([P, G], F32, name="nm")
+        z = keep.tile([P, G], F32, name="z")
+        comb, comb_sb = {}, keep.tile([1, G * OUT], F32, name="comb_sb", align_bytes=64)
+        inv = 1.0 / OUT
+        pms = {}
+
+        def span(g):
+            return T0[groups[g][0]], T0[groups[g][1] - 1] + SIZES[groups[g][1] - 1]
+
+        def softmax_pm(g):
+            a, b = span(g)
+            pms[g] = small.tile([P, 1], F32, name="pm")
+            nc.vector.reduce_max(out=pms[g][:], in_=ss[:, a:b], axis=X)
+
+        def softmax_max(g):
+            mx = tps.tile([P, 512], F32, name="tp_t")
+            nc.tensor.transpose(mx[:, 0:P], pms[g][:].to_broadcast([P, P]), ident[:])
+            nc.vector.reduce_max(out=gm[:, g:g + 1], in_=mx[:, 0:P], axis=X)
+            nc.vector.tensor_scalar(out=nm[:, g:g + 1], in0=gm[:, g:g + 1], scalar1=-inv, scalar2=None, op0=MULT)
+
+        def softmax_exp(g):
+            a, b = span(g)
+            nc.scalar.activation(out=e[:, a:b], in_=ss[:, a:b], func=ACT.Exp, scale=inv, bias=nm[:, g:g + 1],
+                                 accum_out=z[:, g:g + 1])
+
+        def ematmul(c, j):
+            g = [k for k in range(G) if groups[k][0] <= c < groups[k][1]][0]
+            a, b = span(g)
+            i = T0[c] + j
+            if i == a:
+                comb[g] = cps.tile([P, OUT], F32, name="comb")
+            nc.tensor.matmul(out=comb[g][:], lhsT=e[:, i:i + 1].to_broadcast([P, P]),
+                             rhs=diff[c][:, j * OUT:(j + 1) * OUT], start=(i == a), stop=(i == b - 1))
+            if i == b - 1:
+                nc.scalar.copy(out=comb_sb[:, g * OUT:(g + 1) * OUT], in_=comb[g][0:1, :])
+
+        dr = keep.tile([P, 8], F32, name="dr")
+        wg, w1tp = [], {}
+
+        def w1_turn(n, h):
+            if h == 0:
+                wg.append(keep.tile([P, 4 * K], BF16, name="w1g%d" % n, align_bytes=64))
+            tp_t, = transpose_words(w1raw[n][:, h * 1024:(h + 1) * 1024], 2)
+            words_out("s", tp_t, wg[n][:, h * 1024:(h + 1) * 1024])
+
+        def w1_quant(n):
+            w1q[n] = keep.tile([P, HID], U32, name="w1q%d" % n, align_bytes=64)
+            w1s[n] = keep.tile([P, HID], U8, name="w1s%d" % n, align_bytes=64)
+            nc.vector.quantize_mx(out=w1q[n][:].bitcast(FP8X4), scales=w1s[n][:], in_=wg[n][:])
+
+        B(0)
+        C(0)
+        B(1, 0, 2)
+        nc.scalar.copy(out=scale4[:, K:2 * K], in_=scale4[:, 0:K])
+        nc.scalar.copy(out=scale4[:, 2 * K:4 * K], in_=scale4[:, 0:2 * K])
+        D(0, 0)
+        w1_turn(0, 0)
+        w1_turn(0, 1)
+        E(0)
+        B(1, 2, 3)
+        w1_quant(0)
+        B(1, 3, 4)
+        w1_turn(1, 0)
+        w1_turn(1, 1)
+        for n in range(2):
+            nc.vector.tensor_copy(out=dr[:, 4 * n:4 * n + 4], in_=dr_raw[n][:])
+        w1_quant(1)
+        w2n = keep.tile([P, HID], BF16, name="w2n", align_bytes=64)
+        b2 = keep.tile([P, OUT], F32, name="b2", align_bytes=64)
+        w2g = keep.tile([P, 2 * HID], BF16, name="w2g", align_bytes=64)
+        w2q = keep.tile([P, 2 * OUT], U32, name="w2q", align_bytes=64)
+        w2s = keep.tile([P, 2 * OUT], U8, name="w2s", align_bytes=64)
+
+        def w2_prep():
+            nc.vector.tensor_scalar(out=w2n[:], in0=w2raw[1][:], scalar1=-1.0, scalar2=None, op0=MULT)
+            nc.vector.tensor_tensor(out=b2[:], in0=b_raw[0][:], in1=b_raw[1][:], op=SUB)
+            tp_t = tps.tile([P, 512], F32, name="tp_t")
+            for n in range(2):
+                words = (w2raw[0] if n == 0 else w2n)[:].bitcast(F32)
+                for u in range(2):
+                    nc.tensor.transpose(tp_t[:, (2 * n + u) * P:(2 * n + u + 1) * P], words[:, u:256:2], ident[:])
+            words_out("s", tp_t, w2g[:])
+
+        pending = []
+        ready = None
+        for c in range(0, NC + 2):
+            run, prev, old = c < NC, 0 <= c - 1 < NC, 0 <= c - 2 < NC
+            last = c - 1 == NC - 1
+            if 0 < c < NC - 1:
+                C(c + 1)
+            hs = 0 if not prev else (128 if last else HS * SIZES[c - 1] // 4)
+            if prev:
+                H(c - 1, 0, hs)
+            if c == 0:
+                for t in range(4):
+                    FG(c, 0, t)
+                C(c + 1)
+            for t in range(2):
+                if run and c:
+                    FG(c, 0, t)
+                if c + 1 < NC:
+                    D(c + 1, t)
+            if c + 2 < NC:
+                B(c + 2)
+            if c + 1 < NC:
+                E(c + 1)
+            if ready is not None:
+                softmax_pm(ready)
+            if prev:
+                I(c - 1, 0)
+            for t in range(2, 4):
+                if run and c:
+                    FG(c, 0, t)
+            if c == 0:
+                w2_prep()
+            if prev:
+                H(c - 1, 1, hs)
+            if old:
+                J(c - 2)
+                Kk(c - 2)
+            if ready is not None:
+                softmax_max(ready)
+            for t in range(4):
+                if run:
+                    FG(c, 1, t)
+                for ck, j in pending[:2]:
+                    ematmul(ck, j)
+                pending = pending[2:]
+            if prev:
+                I(c - 1, 1)
+            if c == 0:
+                nc.vector.quantize_mx(out=w2q[:].bitcast(FP8X4), scales=w2s[:], in_=w2g[:])
+            if ready is not None:
+                softmax_exp(ready)
+                pending += [(ck, j) for ck in range(*groups[ready]) for j in range(SIZES[ck])]
+                ready = None
+            if old:
+                L(c - 2)
+                for g in range(G):
+                    if groups[g][1] - 1 == c - 2:
+                        ready = g
+        softmax_pm(ready)
+        softmax_max(ready)
+        softmax_exp(ready)
+        for ck, j in pending:
+            ematmul(ck, j)
+        for ck in range(*groups[ready]):
+            for j in range(SIZES[ck]):
+                ematmul(ck, j)
+
+        tens = keep.tile([P, Q], F32, name="tens", align_bytes=64)
+        nc.vector.tensor_scalar(out=tens[:], in0=ss[:], scalar1=inv, scalar2=None, op0=MULT)
+        nc.sync.dma_start(out=ot, in_=tens[:])
+        M = keep.tile([P, 1], F32, name="M")
+        nc.vector.reduce_max(out=M[:], in_=gm[:], axis=X)
+        nM = keep.tile([P, 1], F32, name="nM")
+        nc.vector.tensor_scalar(out=nM[:], in0=M[:], scalar1=-inv, scalar2=None, op0=MULT)
+        f = keep.tile([P, G], F32, name="f")
+        nc.scalar.activation(out=f[:], in_=gm[:], func=ACT.Exp, scale=inv, bias=nM[:])
+        sums = keep.tile([P, 2], F32, name="sums")
+        nc.vector.reduce_sum(out=sums[:, 1:2], in_=ss[:], axis=X)
+        zf = keep.tile([P, G], F32, name="zf")
+        nc.vector.tensor_tensor(out=zf[:], in0=z[:], in1=f[:], op=MULT)
+        nc.vector.reduce_sum(out=sums[:, 0:1], in_=zf[:], axis=X)
+        tot = yps.tile([P, WM], F32, name="y_t")
+        nc.tensor.matmul(out=tot[:, 0:2], lhsT=ones[:], rhs=sums[:], start=True, stop=True)
+        rz = keep.tile([1, 1], F32, name="rz")
+        nc.vector.reciprocal(out=rz[:], in_=tot[0:1, 0:1])
+        mt = keep.tile([1, 1], F32, name="mt")
+        nc.vector.tensor_scalar(out=mt[:], in0=tot[0:1, 1:2], scalar1=inv / N, scalar2=None, op0=MULT)
+        nc.sync.dma_start(out=out_3.rearrange("(a b) -> a b", a=1), in_=mt[:])
+        cf = keep.tile([1, OUT * G], F32, name="cf")
+        nc.vector.tensor_tensor(
+            out=cf[:].rearrange("p (g n) -> p g n", g=G), in0=comb_sb[:].rearrange("p (g n) -> p g n", g=G),
+            in1=f[0:1, :].unsqueeze(2).to_broadcast([1, G, OUT]), op=MULT)
+        cs = keep.tile([1, OUT], F32, name="cs")
+        nc.vector.reduce_sum(out=cs[:], in_=cf[:].rearrange("p (g n) -> p n g", g=G), axis=X)
+        cr = keep.tile([1, OUT], F32, name="cr")
+        nc.vector.tensor_scalar(out=cr[:], in0=cs[:], scalar1=rz[:], scalar2=None, op0=MULT)
+        nc.sync.dma_start(out=out_2, in_=cr[:])

@@ -49,7 +49,6 @@ def tile_phiaslossengine_pa_t_kernel(
         hps = ctx.enter_context(tc.psum_pool(name="hps", bufs=4))
         yps = ctx.enter_context(tc.psum_pool(name="yps", bufs=1))
         cps = ctx.enter_context(tc.psum_pool(name="cps", bufs=1))
-        ctx.enter_context(tc.manual_schedule())
 
         hbytes = []
 
@@ -114,18 +113,18 @@ def tile_phiaslossengine_pa_t_kernel(
         def transpose_words(src, nslots):
             words = src.bitcast(F32)
             res = []
-            for h in range(nslots // 2):
+            for h in range((nslots + 1) // 2):
                 tp_t = tps.tile([P, 512], F32, name="tp_t")
-                for j in range(2):
+                for j in range(min(2, nslots - 2 * h)):
                     for u in range(2):
                         s = 256 * (2 * h + j)
                         nc.tensor.transpose(tp_t[:, (2 * j + u) * P:(2 * j + u + 1) * P], words[:, s + u:s + 256:2], ident[:])
                 res.append(tp_t)
             return res
 
-        def words_out(eng, tp_t, dst):
-            o = dst.bitcast(F32).rearrange("p (j r u) -> p j r u", j=2, u=2)
-            i = tp_t[:].rearrange("p (j u r) -> p j r u", j=2, u=2)
+        def words_out(eng, tp_t, dst, slots=2):
+            o = dst.bitcast(F32).rearrange("p (j r u) -> p j r u", j=slots, u=2)
+            i = tp_t[:, 0:slots * 256].rearrange("p (j u r) -> p j r u", j=slots, u=2)
             if eng == "s":
                 nc.scalar.copy(out=o, in_=i)
             else:
@@ -137,7 +136,8 @@ def tile_phiaslossengine_pa_t_kernel(
 
         def D(c, h, eng="s"):
             if h < len(tp[c]):
-                words_out(eng, tp[c][h], xwords[c][:, h * 1024:(h + 1) * 1024])
+                k = min(2, SIZES[c] - 2 * h)
+                words_out(eng, tp[c][h], xwords[c][:, h * 1024:h * 1024 + k * K], k)
 
         def E(c):
             w = SIZES[c] * P
@@ -203,12 +203,13 @@ def tile_phiaslossengine_pa_t_kernel(
                 nc.scalar.activation(out=junk[:], in_=diff[c][:, j * P:(j + 1) * P], func=ACT.Square,
                                      accum_out=ss[:, T0[c] + j:T0[c] + j + 1])
 
-        groups = [(0, 5), (5, 9), (9, 12), (12, 14), (14, 15), (15, 17)]
+        groups = [(0, 5), (5, 10), (10, 14), (14, 16), (16, 17)]
         G = len(groups)
         gm = keep.tile([P, G], F32, name="gm")
         nm = keep.tile([P, G], F32, name="nm")
         z = keep.tile([P, G], F32, name="z")
-        comb, comb_sb = {}, keep.tile([1, G * OUT], F32, name="comb_sb", align_bytes=64)
+        comb_t = cps.tile([P, 4 * OUT], F32, name="comb")
+        comb = {g: comb_t[:, g * OUT:(g + 1) * OUT] for g in range(G - 1)}
         inv = 1.0 / OUT
         pms = {}
 
@@ -235,12 +236,9 @@ def tile_phiaslossengine_pa_t_kernel(
             g = [k for k in range(G) if groups[k][0] <= c < groups[k][1]][0]
             a, b = span(g)
             i = T0[c] + j
-            if i == a:
-                comb[g] = cps.tile([P, OUT], F32, name="comb")
-            nc.tensor.matmul(out=comb[g][:], lhsT=e[:, i:i + 1].to_broadcast([P, P]),
+            nc.tensor.matmul(out=comb[g], lhsT=e[:, i:i + 1].to_broadcast([P, P]),
                              rhs=diff[c][:, j * OUT:(j + 1) * OUT], start=(i == a), stop=(i == b - 1))
-            if i == b - 1:
-                nc.scalar.copy(out=comb_sb[:, g * OUT:(g + 1) * OUT], in_=comb[g][0:1, :])
+
 
         dr = keep.tile([P, 8], F32, name="dr")
         wg, w1tp = [], {}
@@ -347,42 +345,50 @@ def tile_phiaslossengine_pa_t_kernel(
                 for g in range(G):
                     if groups[g][1] - 1 == c - 2:
                         ready = g
-        softmax_pm(ready)
-        softmax_max(ready)
-        softmax_exp(ready)
-        for ck, j in pending:
-            ematmul(ck, j)
-        for ck in range(*groups[ready]):
-            for j in range(SIZES[ck]):
-                ematmul(ck, j)
-
+        GL = G - 1
+        f = keep.tile([P, G], F32, name="f")
+        nc.gpsimd.memset(f[:, GL:G], 1.0)
+        sums = keep.tile([P, 2], F32, name="sums")
         tens = keep.tile([P, Q], F32, name="tens", align_bytes=64)
+        softmax_pm(GL)
         nc.vector.tensor_scalar(out=tens[:], in0=ss[:], scalar1=inv, scalar2=None, op0=MULT)
         nc.sync.dma_start(out=ot, in_=tens[:])
+        nc.vector.reduce_sum(out=sums[:, 1:2], in_=ss[:], axis=X)
+        mx = tps.tile([P, 512], F32, name="tp_t")
+        nc.tensor.transpose(mx[:, 0:P], pms[GL][:].to_broadcast([P, P]), ident[:])
+        nc.vector.reduce_max(out=gm[:, GL:G], in_=mx[:, 0:P], axis=X)
         M = keep.tile([P, 1], F32, name="M")
         nc.vector.reduce_max(out=M[:], in_=gm[:], axis=X)
         nM = keep.tile([P, 1], F32, name="nM")
         nc.vector.tensor_scalar(out=nM[:], in0=M[:], scalar1=-inv, scalar2=None, op0=MULT)
-        f = keep.tile([P, G], F32, name="f")
-        nc.scalar.activation(out=f[:], in_=gm[:], func=ACT.Exp, scale=inv, bias=nM[:])
-        sums = keep.tile([P, 2], F32, name="sums")
-        nc.vector.reduce_sum(out=sums[:, 1:2], in_=ss[:], axis=X)
+        a, b = span(GL)
+        nc.scalar.activation(out=e[:, a:b], in_=ss[:, a:b], func=ACT.Exp, scale=inv, bias=nM[:], accum_out=z[:, GL:G])
+        nc.scalar.activation(out=f[:, 0:GL], in_=gm[:, 0:GL], func=ACT.Exp, scale=inv, bias=nM[:])
+        for ck, j in pending:
+            ematmul(ck, j)
+        last = tps.tile([P, 512], F32, name="tp_t")
+        comb[GL] = last[:, 0:OUT]
+        for ck in range(*groups[GL]):
+            for j in range(SIZES[ck]):
+                ematmul(ck, j)
         zf = keep.tile([P, G], F32, name="zf")
         nc.vector.tensor_tensor(out=zf[:], in0=z[:], in1=f[:], op=MULT)
+        cf = keep.tile([1, OUT * GL], F32, name="cf")
+        nc.vector.tensor_tensor(
+            out=cf[:].rearrange("p (g n) -> p g n", g=GL), in0=comb_t[0:1, 0:GL * OUT].rearrange("p (g n) -> p g n", g=GL),
+            in1=f[0:1, 0:GL].unsqueeze(2).to_broadcast([1, GL, OUT]), op=MULT)
         nc.vector.reduce_sum(out=sums[:, 0:1], in_=zf[:], axis=X)
         tot = yps.tile([P, WM], F32, name="y_t")
         nc.tensor.matmul(out=tot[:, 0:2], lhsT=ones[:], rhs=sums[:], start=True, stop=True)
+        cs = keep.tile([1, OUT], F32, name="cs")
+        nc.vector.reduce_sum(out=cs[:], in_=cf[:].rearrange("p (g n) -> p n g", g=GL), axis=X)
         rz = keep.tile([1, 1], F32, name="rz")
         nc.vector.reciprocal(out=rz[:], in_=tot[0:1, 0:1])
         mt = keep.tile([1, 1], F32, name="mt")
         nc.vector.tensor_scalar(out=mt[:], in0=tot[0:1, 1:2], scalar1=inv / N, scalar2=None, op0=MULT)
         nc.sync.dma_start(out=out_3.rearrange("(a b) -> a b", a=1), in_=mt[:])
-        cf = keep.tile([1, OUT * G], F32, name="cf")
-        nc.vector.tensor_tensor(
-            out=cf[:].rearrange("p (g n) -> p g n", g=G), in0=comb_sb[:].rearrange("p (g n) -> p g n", g=G),
-            in1=f[0:1, :].unsqueeze(2).to_broadcast([1, G, OUT]), op=MULT)
-        cs = keep.tile([1, OUT], F32, name="cs")
-        nc.vector.reduce_sum(out=cs[:], in_=cf[:].rearrange("p (g n) -> p n g", g=G), axis=X)
+        cz = keep.tile([1, OUT], F32, name="cz")
+        nc.vector.tensor_scalar(out=cz[:], in0=cs[:], scalar1=rz[:], scalar2=None, op0=MULT)
         cr = keep.tile([1, OUT], F32, name="cr")
-        nc.vector.tensor_scalar(out=cr[:], in0=cs[:], scalar1=rz[:], scalar2=None, op0=MULT)
+        nc.vector.scalar_tensor_tensor(out=cr[:], in0=last[0:1, 0:OUT], scalar=rz[:], in1=cz[:], op0=MULT, op1=ADD)
         nc.sync.dma_start(out=out_2, in_=cr[:])

from contextlib import ExitStack

import concourse.mybir as mybir
from concourse.masks import make_identity

F32 = mybir.dt.float32
BF16 = mybir.dt.bfloat16
U32 = mybir.dt.uint32
U8 = mybir.dt.uint8
FP8 = mybir.dt.float8_e4m3fn
FP8X4 = mybir.dt.float8_e4m3fn_x4
ADD = mybir.AluOpType.add
SUB = mybir.AluOpType.subtract
MULT = mybir.AluOpType.mult
MAX = mybir.AluOpType.max
ACT = mybir.ActivationFunctionType
X = mybir.AxisListType.X

P = 128
N, K, HID, OUT = 8192, 512, 512, 128
Q = N // P
SIZES = [2] + [4] * 15 + [2]
NC = len(SIZES)
T0 = [sum(SIZES[:c]) for c in range(NC)]
CTM = 4
WM = CTM * P
HS = 56

FLOPS = 2 * N * K * 2 * HID + 2 * N * 2 * HID * OUT


def tile_phiaslossengine_pa_t_kernel(
    tc, hiddens_bytes, hiddens_scale, Wa1h, drive_a, Wa2, ba2, Wg1h, drive_g, Wg2, bg2,
    out_0, out_1, out_2, out_3,
):
    nc = tc.nc
    hb = hiddens_bytes.rearrange("(p q) k -> p (q k)", q=Q)
    od = out_0.rearrange("(p q) n -> p (q n)", q=Q)
    ot = out_1.rearrange("(p q) o -> p (q o)", q=Q)

    with ExitStack() as ctx:
        keep = ctx.enter_context(tc.tile_pool(name="keep", bufs=1))
        bpool = ctx.enter_context(tc.tile_pool(name="bytes", bufs=NC))
        xpool = ctx.enter_context(tc.tile_pool(name="x", bufs=3))
        upool = ctx.enter_context(tc.tile_pool(name="u", bufs=4))
        dpool = ctx.enter_context(tc.tile_pool(name="d", bufs=NC))
        small = ctx.enter_context(tc.tile_pool(name="small", bufs=2))
        tps = ctx.enter_context(tc.psum_pool(name="tps", bufs=2))
        hps = ctx.enter_context(tc.psum_pool(name="hps", bufs=4))
        yps = ctx.enter_context(tc.psum_pool(name="yps", bufs=1))
        cps = ctx.enter_context(tc.psum_pool(name="cps", bufs=1))

        hbytes = []

        def load(c):
            hb_t = bpool.tile([P, CTM * K], U8, name="hb_t", align_bytes=64)
            nc.sync.dma_start(out=hb_t[:, 0:SIZES[c] * K], in_=hb[:, T0[c] * K:(T0[c] + SIZES[c]) * K])
            hbytes.append(hb_t)

        scale4 = keep.tile([P, CTM * K], F32, name="scale4", align_bytes=64)
        nc.scalar.dma_start(out=scale4[:, 0:K], in_=hiddens_scale.rearrange("o k -> (o k)").partition_broadcast(P))
        load(0)
        w1raw = []
        for n, w in enumerate((Wa1h, Wg1h)):
            wr = keep.tile([P, 4 * K], BF16, name="w1raw%d" % n, align_bytes=64)
            nc.sync.dma_start(out=wr[:].rearrange("p (t k) -> p t k", t=4), in_=w.rearrange("(m t) k -> m t k", t=4))
            w1raw.append(wr)
            load(1 + n)
        dr_raw = []
        for n, v in enumerate((drive_a, drive_g)):
            t_ = keep.tile([P, 4], BF16, name="drraw%d" % n)
            nc.scalar.dma_start(out=t_[:], in_=v.rearrange("(p t) -> p t", t=4))
            dr_raw.append(t_)
        w2raw = []
        for n, w in enumerate((Wa2, Wg2)):
            wr = keep.tile([P, HID], BF16, name="w2raw%d" % n, align_bytes=64)
            nc.sync.dma_start(out=wr[:], in_=w)
            w2raw.append(wr)
        b_raw = []
        for n, v in enumerate((ba2, bg2)):
            t_ = keep.tile([P, OUT], BF16, name="braw%d" % n, align_bytes=64)
            nc.sync.dma_start(out=t_[:], in_=v.partition_broadcast(P))
            b_raw.append(t_)
        for c in range(3, NC):
            load(c)

        ident = keep.tile([P, P], F32, name="ident", align_bytes=64)
        make_identity(nc, ident[:])
        ones = keep.tile([P, P], F32, name="ones", align_bytes=64)
        nc.gpsimd.memset(ones[:], 1.0)
        warm = keep.tile([P, 1], F32, name="warm")
        nc.gpsimd.memset(warm[:], 0.0)
        warm2 = keep.tile([P, 1], F32, name="warm2")
        nc.scalar.activation(out=warm2[:], in_=warm[:], func=ACT.Exp)

        ss = keep.tile([P, Q], F32, name="ss", align_bytes=64)
        e = keep.tile([P, Q], F32, name="e", align_bytes=64)

        xs, xwords, xq, xsc, tp = {}, {}, {}, {}, {}
        up, ug, uq, us = {}, {}, {}, {}
        diff = {}
        w1q, w1s = [None, None], [None, None]

        def B(c, a=None, b=None):
            n = SIZES[c] * K
            if not a:
                xs[c] = xpool.tile([P, CTM * K], BF16, name="xs", align_bytes=64)
            step = K if c < 2 else n
            for s in range((a or 0) * K, n if b is None else b * K, step):
                nc.vector.tensor_tensor(out=xs[c][:, s:s + step], in0=hbytes[c][:, s:s + step].bitcast(FP8),
                                        in1=scale4[:, 0:step], op=MULT)

        def transpose_words(src, nslots):
            words = src.bitcast(F32)
            res = []
            for h in range((nslots + 1) // 2):
                tp_t = tps.tile([P, 512], F32, name="tp_t")
                for j in range(min(2, nslots - 2 * h)):
                    for u in range(2):
                        s = 256 * (2 * h + j)
                        nc.tensor.transpose(tp_t[:, (2 * j + u) * P:(2 * j + u + 1) * P], words[:, s + u:s + 256:2], ident[:])
                res.append(tp_t)
            return res

        def words_out(eng, tp_t, dst, slots=2):
            o = dst.bitcast(F32).rearrange("p (j r u) -> p j r u", j=slots, u=2)
            i = tp_t[:, 0:slots * 256].rearrange("p (j u r) -> p j r u", j=slots, u=2)
            if eng == "s":
                nc.scalar.copy(out=o, in_=i)
            else:
                nc.vector.tensor_copy(out=o, in_=i)

        def C(c):
            tp[c] = transpose_words(xs.pop(c)[:], SIZES[c])
            xwords[c] = xpool.tile([P, CTM * K], BF16, name="xg", align_bytes=64)

        def D(c, h, eng="s"):
            if h < len(tp[c]):
                k = min(2, SIZES[c] - 2 * h)
                words_out(eng, tp[c][h], xwords[c][:, h * 1024:h * 1024 + k * K], k)

        def E(c):
            w = SIZES[c] * P
            xq[c] = xpool.tile([P, WM], U32, name="xq", align_bytes=64)
            xsc[c] = xpool.tile([P, WM], U8, name="xsc", align_bytes=64)
            nc.vector.quantize_mx(out=xq[c][:, 0:w].bitcast(FP8X4), scales=xsc[c][:, 0:w], in_=xwords.pop(c)[:, 0:4 * w])

        def FG(c, n, t, eng="s"):
            w = SIZES[c] * P
            if t == 0:
                up[c, n] = upool.tile([P, 4 * WM], BF16, name="up", align_bytes=64)
            h_t = hps.tile([P, WM], F32, name="h_t")
            nc.tensor.matmul_mx(
                out=h_t[:, 0:w],
                lhsT=w1q[n][:, t * P:(t + 1) * P].bitcast(FP8X4), lhsT_scale=w1s[n][:, t * P:(t + 1) * P],
                rhs=xq[c][:, 0:w].bitcast(FP8X4), rhs_scale=xsc[c][:, 0:w], start=True, stop=True)
            o = up[c, n][:, t * w:(t + 1) * w]
            b = dr[:, 4 * n + t:4 * n + t + 1]
            if eng == "s":
                nc.scalar.activation(out=o, in_=h_t[:, 0:w], func=ACT.Relu, bias=b)
            else:
                nc.vector.tensor_scalar(out=o, in0=h_t[:, 0:w], scalar1=b, scalar2=0.0, op0=ADD, op1=MAX)

        def H(c, n, hs):
            w = SIZES[c] * P
            ug[c, n] = upool.tile([P, 4 * WM], BF16, name="ug", align_bytes=64)
            dst = ug[c, n][:, 0:4 * w].rearrange("p (c i t) -> p c t i", i=4, t=4)
            src = up.pop((c, n))[:, 0:4 * w].rearrange("p (t c i) -> p c t i", t=4, i=4)
            cut = (w - hs) // 4
            if hs:
                nc.scalar.copy(out=dst[:, cut:w // 4], in_=src[:, cut:w // 4])
            nc.vector.tensor_copy(out=dst[:, 0:cut], in_=src[:, 0:cut])

        def I(c, n):
            w = SIZES[c] * P
            uq[c, n] = upool.tile([P, WM], U32, name="uq", align_bytes=64)
            us[c, n] = upool.tile([P, WM], U8, name="us", align_bytes=64)
            nc.vector.quantize_mx(out=uq[c, n][:, 0:w].bitcast(FP8X4), scales=us[c, n][:, 0:w], in_=ug.pop((c, n))[:, 0:4 * w])

        y = {}

        def J(c):
            y[c] = yps.tile([P, WM], F32, name="y_t")
            for j in range(SIZES[c]):
                for n in range(2):
                    nc.tensor.matmul_mx(
                        out=y[c][:, j * P:(j + 1) * P],
                        lhsT=uq[c, n][:, j * P:(j + 1) * P].bitcast(FP8X4), lhsT_scale=us[c, n][:, j * P:(j + 1) * P],
                        rhs=w2q[:, n * P:(n + 1) * P].bitcast(FP8X4), rhs_scale=w2s[:, n * P:(n + 1) * P],
                        start=(n == 0), stop=(n == 1))

        def Kk(c):
            w = SIZES[c] * P
            diff[c] = dpool.tile([P, WM], F32, name="diff", align_bytes=64)
            nc.vector.tensor_tensor(
                out=diff[c][:, 0:w].rearrange("p (j n) -> p j n", n=OUT), in0=y.pop(c)[:, 0:w].rearrange("p (j n) -> p j n", n=OUT),
                in1=b2[:].unsqueeze(1).to_broadcast([P, SIZES[c], OUT]), op=ADD)
            nc.sync.dma_start(out=od[:, T0[c] * OUT:(T0[c] + SIZES[c]) * OUT], in_=diff[c][:, 0:w])

        def L(c):
            for j in range(SIZES[c]):
                junk = small.tile([P, OUT], F32, name="junk")
                nc.scalar.activation(out=junk[:], in_=diff[c][:, j * P:(j + 1) * P], func=ACT.Square,
                                     accum_out=ss[:, T0[c] + j:T0[c] + j + 1])

        groups = [(0, 5), (5, 10), (10, 14), (14, 16), (16, 17)]
        G = len(groups)
        gm = keep.tile([P, G], F32, name="gm")
        nm = keep.tile([P, G], F32, name="nm")
        z = keep.tile([P, G], F32, name="z")
        comb_t = cps.tile([P, 4 * OUT], F32, name="comb")
        comb = {g: comb_t[:, g * OUT:(g + 1) * OUT] for g in range(G - 1)}
        inv = 1.0 / OUT
        pms = {}

        def span(g):
            return T0[groups[g][0]], T0[groups[g][1] - 1] + SIZES[groups[g][1] - 1]

        def softmax_pm(g):
            a, b = span(g)
            pms[g] = small.tile([P, 1], F32, name="pm")
            nc.vector.reduce_max(out=pms[g][:], in_=ss[:, a:b], axis=X)

        def softmax_max(g):
            mx = tps.tile([P, 512], F32, name="tp_t")
            nc.tensor.transpose(mx[:, 0:P], pms[g][:].to_broadcast([P, P]), ident[:])
            nc.vector.reduce_max(out=gm[:, g:g + 1], in_=mx[:, 0:P], axis=X)
            nc.vector.tensor_scalar(out=nm[:, g:g + 1], in0=gm[:, g:g + 1], scalar1=-inv, scalar2=None, op0=MULT)

        def softmax_exp(g):
            a, b = span(g)
            nc.scalar.activation(out=e[:, a:b], in_=ss[:, a:b], func=ACT.Exp, scale=inv, bias=nm[:, g:g + 1],
                                 accum_out=z[:, g:g + 1])

        def ematmul(c, j):
            g = [k for k in range(G) if groups[k][0] <= c < groups[k][1]][0]
            a, b = span(g)
            i = T0[c] + j
            nc.tensor.matmul(out=comb[g], lhsT=e[:, i:i + 1].to_broadcast([P, P]),
                             rhs=diff[c][:, j * OUT:(j + 1) * OUT], start=(i == a), stop=(i == b - 1))


        dr = keep.tile([P, 8], F32, name="dr")
        wg, w1tp = [], {}

        def w1_turn(n, h):
            if h == 0:
                wg.append(keep.tile([P, 4 * K], BF16, name="w1g%d" % n, align_bytes=64))
            tp_t, = transpose_words(w1raw[n][:, h * 1024:(h + 1) * 1024], 2)
            words_out("s", tp_t, wg[n][:, h * 1024:(h + 1) * 1024])

        def w1_quant(n):
            w1q[n] = keep.tile([P, HID], U32, name="w1q%d" % n, align_bytes=64)
            w1s[n] = keep.tile([P, HID], U8, name="w1s%d" % n, align_bytes=64)
            nc.vector.quantize_mx(out=w1q[n][:].bitcast(FP8X4), scales=w1s[n][:], in_=wg[n][:])

        B(0)
        C(0)
        B(1, 0, 2)
        nc.scalar.copy(out=scale4[:, K:2 * K], in_=scale4[:, 0:K])
        nc.scalar.copy(out=scale4[:, 2 * K:4 * K], in_=scale4[:, 0:2 * K])
        D(0, 0)
        w1_turn(0, 0)
        w1_turn(0, 1)
        E(0)
        B(1, 2, 3)
        w1_quant(0)
        B(1, 3, 4)
        w1_turn(1, 0)
        w1_turn(1, 1)
        for n in range(2):
            nc.vector.tensor_copy(out=dr[:, 4 * n:4 * n + 4], in_=dr_raw[n][:])
        w1_quant(1)
        w2n = keep.tile([P, HID], BF16, name="w2n", align_bytes=64)
        b2 = keep.tile([P, OUT], F32, name="b2", align_bytes=64)
        w2g = keep.tile([P, 2 * HID], BF16, name="w2g", align_bytes=64)
        w2q = keep.tile([P, 2 * OUT], U32, name="w2q", align_bytes=64)
        w2s = keep.tile([P, 2 * OUT], U8, name="w2s", align_bytes=64)

        def w2_prep():
            nc.vector.tensor_scalar(out=w2n[:], in0=w2raw[1][:], scalar1=-1.0, scalar2=None, op0=MULT)
            nc.vector.tensor_tensor(out=b2[:], in0=b_raw[0][:], in1=b_raw[1][:], op=SUB)
            tp_t = tps.tile([P, 512], F32, name="tp_t")
            for n in range(2):
                words = (w2raw[0] if n == 0 else w2n)[:].bitcast(F32)
                for u in range(2):
                    nc.tensor.transpose(tp_t[:, (2 * n + u) * P:(2 * n + u + 1) * P], words[:, u:256:2], ident[:])
            words_out("s", tp_t, w2g[:])

        pending = []
        ready = None
        for c in range(0, NC + 2):
            run, prev, old = c < NC, 0 <= c - 1 < NC, 0 <= c - 2 < NC
            last = c - 1 == NC - 1
            if 0 < c < NC - 1:
                C(c + 1)
            hs = 0 if not prev else (128 if last else HS * SIZES[c - 1] // 4)
            if prev:
                H(c - 1, 0, hs)
            if c == 0:
                for t in range(4):
                    FG(c, 0, t)
                C(c + 1)
            for t in range(2):
                if run and c:
                    FG(c, 0, t)
                if c + 1 < NC:
                    D(c + 1, t)
            if c + 2 < NC:
                B(c + 2)
            if c + 1 < NC:
                E(c + 1)
            if ready is not None:
                softmax_pm(ready)
            if prev:
                I(c - 1, 0)
            for t in range(2, 4):
                if run and c:
                    FG(c, 0, t)
            if c == 0:
                w2_prep()
            if prev:
                H(c - 1, 1, hs)
            if old:
                J(c - 2)
                Kk(c - 2)
            if ready is not None:
                softmax_max(ready)
            for t in range(4):
                if run:
                    FG(c, 1, t)
                for ck, j in pending[:2]:
                    ematmul(ck, j)
                pending = pending[2:]
            if prev:
                I(c - 1, 1)
            if c == 0:
                nc.vector.quantize_mx(out=w2q[:].bitcast(FP8X4), scales=w2s[:], in_=w2g[:])
            if ready is not None:
                softmax_exp(ready)
                pending += [(ck, j) for ck in range(*groups[ready]) for j in range(SIZES[ck])]
                ready = None
            if old:
                L(c - 2)
                for g in range(G):
                    if groups[g][1] - 1 == c - 2:
                        ready = g
        GL = G - 1
        f = keep.tile([P, G], F32, name="f")
        nc.gpsimd.memset(f[:, GL:G], 1.0)
        sums = keep.tile([P, 2], F32, name="sums")
        tens = keep.tile([P, Q], F32, name="tens", align_bytes=64)
        softmax_pm(GL)
        nc.vector.tensor_scalar(out=tens[:], in0=ss[:], scalar1=inv, scalar2=None, op0=MULT)
        nc.sync.dma_start(out=ot, in_=tens[:])
        nc.vector.reduce_sum(out=sums[:, 1:2], in_=ss[:], axis=X)
        mx = tps.tile([P, 512], F32, name="tp_t")
        nc.tensor.transpose(mx[:, 0:P], pms[GL][:].to_broadcast([P, P]), ident[:])
        nc.vector.reduce_max(out=gm[:, GL:G], in_=mx[:, 0:P], axis=X)
        M = keep.tile([P, 1], F32, name="M")
        nc.vector.reduce_max(out=M[:], in_=gm[:], axis=X)
        nM = keep.tile([P, 1], F32, name="nM")
        nc.vector.tensor_scalar(out=nM[:], in0=M[:], scalar1=-inv, scalar2=None, op0=MULT)
        a, b = span(GL)
        nc.scalar.activation(out=e[:, a:b], in_=ss[:, a:b], func=ACT.Exp, scale=inv, bias=nM[:], accum_out=z[:, GL:G])
        nc.scalar.activation(out=f[:, 0:GL], in_=gm[:, 0:GL], func=ACT.Exp, scale=inv, bias=nM[:])
        for ck, j in pending:
            ematmul(ck, j)
        last = tps.tile([P, 512], F32, name="tp_t")
        comb[GL] = last[:, 0:OUT]
        for ck in range(*groups[GL]):
            for j in range(SIZES[ck]):
                ematmul(ck, j)
        zf = keep.tile([P, G], F32, name="zf")
        nc.vector.tensor_tensor(out=zf[:], in0=z[:], in1=f[:], op=MULT)
        cf = keep.tile([1, OUT * GL], F32, name="cf")
        nc.vector.tensor_tensor(
            out=cf[:].rearrange("p (g n) -> p g n", g=GL), in0=comb_t[0:1, 0:GL * OUT].rearrange("p (g n) -> p g n", g=GL),
            in1=f[0:1, 0:GL].unsqueeze(2).to_broadcast([1, GL, OUT]), op=MULT)
        nc.vector.reduce_sum(out=sums[:, 0:1], in_=zf[:], axis=X)
        tot = yps.tile([P, WM], F32, name="y_t")
        nc.tensor.matmul(out=tot[:, 0:2], lhsT=ones[:], rhs=sums[:], start=True, stop=True)
        cs = keep.tile([1, OUT], F32, name="cs")
        nc.vector.reduce_sum(out=cs[:], in_=cf[:].rearrange("p (g n) -> p n g", g=GL), axis=X)
        rz = keep.tile([1, 1], F32, name="rz")
        nc.vector.reciprocal(out=rz[:], in_=tot[0:1, 0:1])
        mt = keep.tile([1, 1], F32, name="mt")
        nc.vector.tensor_scalar(out=mt[:], in0=tot[0:1, 1:2], scalar1=inv / N, scalar2=None, op0=MULT)
        nc.sync.dma_start(out=out_3.rearrange("(a b) -> a b", a=1), in_=mt[:])
        cz = keep.tile([1, OUT], F32, name="cz")
        nc.vector.tensor_scalar(out=cz[:], in0=cs[:], scalar1=rz[:], scalar2=None, op0=MULT)
        cr = keep.tile([1, OUT], F32, name="cr")
        nc.vector.scalar_tensor_tensor(out=cr[:], in0=last[0:1, 0:OUT], scalar=rz[:], in1=cz[:], op0=MULT, op1=ADD)
        nc.sync.dma_start(out=out_2, in_=cr[:])
